import numpy as np
import ml_dtypes


def mxq(x, axis, fmt="e4m3"):
    dtype, down = {"e4m3": (ml_dtypes.float8_e4m3fn, 7), "e5m2": (ml_dtypes.float8_e5m2, 14)}[fmt]
    v = np.moveaxis(np.asarray(x, np.float32).astype(ml_dtypes.bfloat16).astype(np.float64), axis, -1)
    blocks = v.reshape(v.shape[:-1] + (-1, 32))
    amax = np.abs(blocks).max(-1, keepdims=True)
    byte = np.maximum(np.where(amax > 0, np.frexp(amax)[1] - 1 + 127, 0) - down, 1)
    scale = np.exp2(byte - 127.0)
    codes = (blocks / scale).astype(np.float32).astype(dtype).astype(np.float64)
    return np.moveaxis((codes * scale).reshape(v.shape), -1, axis)


WIDE = False


def mx_kscale(k):
    if not WIDE:
        return np.ones(k)
    levels = np.array([30, -30])
    if k % 512:
        return np.exp2(np.random.permutation(np.resize(levels, k // 32))).repeat(32)
    a = np.empty((k // 512, 16))
    for p in range(k // 512):
        a[p, :8] = np.random.permutation(np.resize(levels, 8))
        for g in range(8):
            far = levels[np.abs(levels - a[p, g]) >= 10]
            a[p, g + 8] = far[np.random.randint(len(far))]
    return np.exp2(a.ravel()).repeat(32)


BF16 = ml_dtypes.bfloat16


def bf(x):
    return np.asarray(x, np.float32).astype(BF16)


def f64(x):
    return np.asarray(x).astype(np.float64)


B, SIDE, HE, Z, HD, XO = 1024, 32, 1024, 512, 2048, 1024


def setup_inputs():
    n = np.random.standard_normal
    s = mx_kscale(HD)
    return {"hd": bf(np.tanh(n((B, HD))) * s),
            "W_mu_d": bf(n((XO, HD)) * 1.5 / np.sqrt(HD) / s[None, :]),
            "b_mu_d": bf(n(XO) * 0.3),
            "W_ls_d": bf(n((XO, HD)) * 1.5 / np.sqrt(HD) / s[None, :]),
            "b_ls_d": bf(n(XO) * 0.3),
            "eps_x": bf(n((B, XO)))}


def reference(hd, W_mu_d, b_mu_d, W_ls_d, b_ls_d, eps_x):
    hq = mxq(f64(hd), 1, "e5m2")
    mu_d = (hq @ mxq(f64(W_mu_d), 1, "e5m2").T) + f64(b_mu_d)
    ls_d = (hq @ mxq(f64(W_ls_d), 1, "e5m2").T) + f64(b_ls_d)
    return mu_d + np.exp(0.5 * ls_d) * f64(eps_x)

@@ -1,0 +1,237 @@
+from contextlib import ExitStack
+
+import concourse.masks as masks
+import concourse.mybir as mybir
+
+B, K, XO = 1024, 2048, 1024
+FLOPS = 2 * 2 * B * K * XO
+
+F32 = mybir.dt.float32
+BF16 = mybir.dt.bfloat16
+U32 = mybir.dt.uint32
+U8 = mybir.dt.uint8
+FP8X4 = mybir.dt.float8_e5m2_x4
+ADD = mybir.AluOpType.add
+MULT = mybir.AluOpType.mult
+EXP = mybir.ActivationFunctionType.Exp
+
+P = 128
+N_TILE = 512
+
+LS0, LS1, MU0, MU1 = 0, 1, 2, 3
+
+
+def halves(ms, q, khs):
+    return [(m, q, kh) for kh in khs for m in ms]
+
+
+def whole(pairs):
+    return [(m, q, kh) for (m, q) in pairs for kh in (0, 1)]
+
+
+RUNS = [
+    ("w", LS0, 0), ("h", 0, 0), ("w", LS0, 1), ("w", LS1, 0), ("w", LS1, 1), ("h", 1, 0),
+    ("h", 2, 0), ("h", 3, 0), ("w", MU0, 0), ("w", MU0, 1), ("w", MU1, 0), ("w", MU1, 1),
+]
+LOAD_SPLIT = [4, 2, 2, 1, 1, 1, 1, 1, 1, 1, 1, 1]
+VECTOR_BANKS = [(1,)] * 12
+PASSES_AFTER_RUN = [
+    [],
+    [],
+    halves((0, 1), LS0, (0,)),
+    halves((0, 1), LS0, (1,)),
+    halves((0, 1), LS1, (0,)),
+    halves((0, 1), LS1, (1,)),
+    whole([(2, LS0), (3, LS0), (2, LS1)]),
+    whole([(3, LS1), (4, LS0), (5, LS0)]),
+    whole([(4, LS1), (5, LS1), (6, LS0)]),
+    whole([(7, LS0), (6, LS1), (7, LS1)]),
+    halves((0, 1, 2, 3), MU0, (0, 1)),
+    halves((4, 5, 6, 7), MU0, (0, 1)) + halves((0, 1, 2, 3), MU1, (0, 1)) + halves((4, 5, 6, 7), MU1, (0, 1)),
+]
+EPS_AFTER_LOAD = {4: 0, 5: 1, 6: 2, 7: 3}
+RAW_BUFS = 6
+WARM = 6
+P_ON_GPSIMD = True
+Q_ON_GPSIMD = True
+
+
+def tile_vae_pb_kernel(tc, hd, W_mu_d, b_mu_d, W_ls_d, b_ls_d, eps_x, out):
+    nc = tc.nc
+    with ExitStack() as ctx:
+        const = ctx.enter_context(tc.tile_pool(name="const", bufs=1))
+        keep = ctx.enter_context(tc.tile_pool(name="keep", bufs=1))
+        raw_pool = ctx.enter_context(tc.tile_pool(name="rawp", bufs=RAW_BUFS))
+        grp_pool = ctx.enter_context(tc.tile_pool(name="grpp", bufs=3))
+        psum = ctx.enter_context(tc.psum_pool(name="psum", bufs=4))
+        ctx.enter_context(tc.manual_schedule())
+
+        ident = const.tile([P, P], F32, name="ident")
+        ones = const.tile([P, P], BF16, name="ones")
+        warm = const.tile([P, N_TILE], BF16, name="warm")
+        brow = const.tile([P, 2 * XO], BF16, name="brow")
+        bias = const.tile([P, 2 * XO], F32, name="bias")
+        tiny = const.tile([P, 2], F32, name="tiny")
+
+        h_codes = keep.tile([P, 4096], U32, name="h_codes", align_bytes=64)
+        h_scales = keep.tile([P, 4096], U8, name="h_scales", align_bytes=64)
+        w_codes = []
+        w_scales = []
+        for q in range(4):
+            wc = keep.tile([P, 2048], U32, name="w_codes%d" % q, align_bytes=64)
+            ws = keep.tile([P, 2048], U8, name="w_scales%d" % q, align_bytes=64)
+            w_codes.append(wc)
+            w_scales.append(ws)
+        eps_sb = []
+        for e in range(4):
+            et = keep.tile([P, 2, XO], BF16, name="eps%d" % e)
+            eps_sb.append(et)
+        res = {}
+        for m in range(8):
+            for h in range(2):
+                rt = keep.tile([P, N_TILE], F32, name="res%d_%d" % (m, h))
+                res[(m, h)] = rt
+
+        nc.vector.memset(ones[:], 1.0)
+        nc.vector.memset(warm[:], 0.0)
+        nc.vector.memset(tiny[:], 0.0)
+        nc.vector.memset(brow[:], 0.0)
+        masks.make_identity(nc, ident[:])
+        nc.scalar.dma_start(out=brow[0:1, 0:XO], in_=b_ls_d.rearrange("(o n) -> o n", o=1))
+        nc.scalar.dma_start(out=brow[0:1, XO : 2 * XO], in_=b_mu_d.rearrange("(o n) -> o n", o=1))
+        nc.scalar.activation(out=tiny[:, 1:2], in_=tiny[:, 0:1], func=EXP)
+
+        raws = {}
+
+        def load(i):
+            kind, a, kh = RUNS[i]
+            raw = raw_pool.tile([P, 4096], BF16, name="raw", tag="raw")
+            raws[i] = raw
+            n = LOAD_SPLIT[i]
+            if kind == "h":
+                src = hd[a * 2 * P : (a + 1) * 2 * P, :].rearrange("(j p) k -> p j k", p=P)
+                dst = raw[:].rearrange("p (j k) -> p j k", j=2)
+                for jj in range(2) if n > 1 else ():
+                    for c in range(n // 2):
+                        ks = slice(c * 2 * K // n, (c + 1) * 2 * K // n)
+                        nc.sync.dma_start(out=dst[:, jj, ks], in_=src[:, jj, ks])
+            else:
+                mat = W_ls_d if a in (LS0, LS1) else W_mu_d
+                r0 = (a % 2) * N_TILE
+                src = mat[r0 : r0 + N_TILE, kh * 1024 : (kh + 1) * 1024].rearrange("(j p) k -> p j k", p=P)
+                dst = raw[:].rearrange("p (j k) -> p j k", j=4)
+                for jh in range(2) if n > 1 else ():
+                    js = slice(2 * jh, 2 * jh + 2)
+                    for c in range(n // 2):
+                        ks = slice(c * 2048 // n, (c + 1) * 2048 // n)
+                        nc.sync.dma_start(out=dst[:, js, ks], in_=src[:, js, ks])
+            if n == 1:
+                nc.sync.dma_start(out=dst, in_=src)
+            if i in EPS_AFTER_LOAD:
+                e = EPS_AFTER_LOAD[i]
+                nc.sync.dma_start(
+                    out=eps_sb[e][:],
+                    in_=eps_x[e * 2 * P : (e + 1) * 2 * P, :].rearrange("(a p) x -> p a x", p=P),
+                )
+
+        def dummy_matmuls(n):
+            acc = psum.tile([P, N_TILE], F32, name="acc", tag="acc")
+            for rep in range(n):
+                nc.tensor.matmul(out=acc[:], lhsT=ones[:], rhs=warm[:], start=True, stop=True)
+
+        def bias_broadcast(c, engine):
+            acc = psum.tile([P, N_TILE], F32, name="acc", tag="acc")
+            cols = slice(c * N_TILE, (c + 1) * N_TILE)
+            nc.tensor.matmul(out=acc[:], lhsT=ones[:], rhs=brow[:, cols], start=True, stop=True)
+            if engine == "v":
+                nc.vector.tensor_copy(out=bias[:, cols], in_=acc[:])
+            else:
+                nc.scalar.copy(out=bias[:, cols], in_=acc[:])
+
+        def transpose_run(i):
+            kind, a, kh = RUNS[i]
+            words = raws[i][:].bitcast(F32)
+            grp = grp_pool.tile([P, 4096], BF16, name="grp", tag="grp", align_bytes=64)
+            banks = []
+            for b in range(4):
+                tp = psum.tile([P, 2, 2, P], F32, name="tp", tag="tp")
+                for s in range(2):
+                    if kind == "w":
+                        c = 4 * (b // 2) + 2 * s + b % 2
+                    else:
+                        c = 4 * (b // 2) + 2 * (b % 2) + s
+                    for u in range(2):
+                        nc.tensor.transpose(tp[:, s, u, :], words[:, 256 * c + u : 256 * (c + 1) : 2], ident[:])
+                banks.append(tp)
+            for b in range(4):
+                blk = 2 * (b % 2) + b // 2 if kind == "w" else b
+                dst = grp[:, 1024 * blk : 1024 * (blk + 1)].bitcast(F32)
+                dst = dst.rearrange("p (s r u) -> p s r u", s=2, u=2)
+                src = banks[b][:].rearrange("p s u r -> p s r u")
+                if b in VECTOR_BANKS[i]:
+                    nc.vector.tensor_copy(out=dst, in_=src)
+                else:
+                    nc.scalar.copy(out=dst, in_=src)
+            if kind == "w":
+                codes, scales, at = w_codes[a], w_scales[a], 1024 * kh
+            else:
+                codes, scales, at = h_codes, h_scales, 1024 * a
+            nc.vector.quantize_mx(
+                out=codes[:, at : at + 1024].bitcast(FP8X4),
+                scales=scales[:, at : at + 1024],
+                in_=grp[:],
+            )
+
+        def finish_ls(m, h):
+            r = res[(m, h)]
+            pe = nc.gpsimd if P_ON_GPSIMD else nc.vector
+            qe = nc.gpsimd if Q_ON_GPSIMD else nc.vector
+            pe.tensor_tensor(out=r[:], in0=r[:], in1=eps_sb[m // 2][:, m % 2, h * N_TILE : (h + 1) * N_TILE], op=MULT)
+            qe.tensor_tensor(out=r[:], in0=r[:], in1=bias[:, XO + h * N_TILE : XO + (h + 1) * N_TILE], op=ADD)
+
+        accs = {}
+
+        def passes(m, q, kh):
+            h = q % 2
+            r = res[(m, h)]
+            if kh == 0:
+                acc = psum.tile([P, N_TILE], F32, name="acc", tag="acc")
+                accs[(m, q)] = acc
+            acc = accs[(m, q)]
+            for g in (2 * kh, 2 * kh + 1):
+                mc = slice(512 * m + P * g, 512 * m + P * (g + 1))
+                nn = slice(N_TILE * g, N_TILE * (g + 1))
+                nc.tensor.matmul_mx(
+                    out=acc[:],
+                    lhsT=h_codes[:, mc].bitcast(FP8X4),
+                    lhsT_scale=h_scales[:, mc],
+                    rhs=w_codes[q][:, nn].bitcast(FP8X4),
+                    rhs_scale=w_scales[q][:, nn],
+                    start=(g == 0),
+                    stop=(g == 3),
+                )
+            if kh == 0:
+                return
+            if q in (LS0, LS1):
+                nc.vector.tensor_tensor(out=r[:], in0=acc[:], in1=bias[:, h * N_TILE : (h + 1) * N_TILE], op=ADD)
+                nc.scalar.activation(out=r[:], in_=r[:], func=EXP, scale=0.5)
+                finish_ls(m, h)
+            else:
+                nc.vector.tensor_tensor(out=r[:], in0=acc[:], in1=r[:], op=ADD)
+                nc.sync.dma_start(out=out[m * P : (m + 1) * P, h * N_TILE : (h + 1) * N_TILE], in_=r[:])
+
+        for i in range(RAW_BUFS):
+            load(i)
+        dummy_matmuls(WARM)
+        for i in range(len(RUNS)):
+            if i >= 1 and i + RAW_BUFS - 1 < len(RUNS):
+                load(i + RAW_BUFS - 1)
+            transpose_run(i)
+            if i == 0:
+                bias_broadcast(0, "v")
+                bias_broadcast(1, "s")
+            if i == 1:
+                bias_broadcast(2, "v")
+                bias_broadcast(3, "s")
+            for job in PASSES_AFTER_RUN[i]:
+                passes(*job)

@@ -34,7 +34,7 @@ RUNS = [
     ("h", 2, 0), ("h", 3, 0), ("w", MU0, 0), ("w", MU0, 1), ("w", MU1, 0), ("w", MU1, 1),
 ]
 LOAD_SPLIT = [4, 2, 2, 1, 1, 1, 1, 1, 1, 1, 1, 1]
-VECTOR_BANKS = [(1,)] * 12
+VECTOR_BANKS = [(1,)] * 3 + [()] * 9
 PASSES_AFTER_RUN = [
     [],
     [],
@@ -52,8 +52,8 @@ PASSES_AFTER_RUN = [
 EPS_AFTER_LOAD = {4: 0, 5: 1, 6: 2, 7: 3}
 RAW_BUFS = 6
 WARM = 6
-P_ON_GPSIMD = True
-Q_ON_GPSIMD = True
+P_ON_GPSIMD = False
+Q_ON_GPSIMD = False
 
 
 def tile_vae_pb_kernel(tc, hd, W_mu_d, b_mu_d, W_ls_d, b_ls_d, eps_x, out):
@@ -64,7 +64,7 @@ def tile_vae_pb_kernel(tc, hd, W_mu_d, b_mu_d, W_ls_d, b_ls_d, eps_x, out):
         raw_pool = ctx.enter_context(tc.tile_pool(name="rawp", bufs=RAW_BUFS))
         grp_pool = ctx.enter_context(tc.tile_pool(name="grpp", bufs=3))
         psum = ctx.enter_context(tc.psum_pool(name="psum", bufs=4))
-        ctx.enter_context(tc.manual_schedule())
+        ctx.enter_context(tc.manual_schedule(engines={mybir.EngineType.PE, mybir.EngineType.SP}))
 
         ident = const.tile([P, P], F32, name="ident")
         ones = const.tile([P, P], BF16, name="ones")

@@ -52,6 +52,8 @@ PASSES_AFTER_RUN = [
 EPS_AFTER_LOAD = {4: 0, 5: 1, 6: 2, 7: 3}
 RAW_BUFS = 6
 WARM = 6
+REORDER_FROM = 9
+RO_AHEAD = 2
 P_ON_GPSIMD = False
 Q_ON_GPSIMD = False
 
@@ -63,6 +65,7 @@ def tile_vae_pb_kernel(tc, hd, W_mu_d, b_mu_d, W_ls_d, b_ls_d, eps_x, out):
         keep = ctx.enter_context(tc.tile_pool(name="keep", bufs=1))
         raw_pool = ctx.enter_context(tc.tile_pool(name="rawp", bufs=RAW_BUFS))
         grp_pool = ctx.enter_context(tc.tile_pool(name="grpp", bufs=3))
+        ro_pool = ctx.enter_context(tc.tile_pool(name="rop", bufs=3))
         psum = ctx.enter_context(tc.psum_pool(name="psum", bufs=4))
         ctx.enter_context(tc.manual_schedule(engines={mybir.EngineType.PE, mybir.EngineType.SP}))
 
@@ -134,6 +137,19 @@ def tile_vae_pb_kernel(tc, hd, W_mu_d, b_mu_d, W_ls_d, b_ls_d, eps_x, out):
                     in_=eps_x[e * 2 * P : (e + 1) * 2 * P, :].rearrange("(a p) x -> p a x", p=P),
                 )
 
+        ordered = {}
+
+        def reorder(i):
+            words = raws[i][:].bitcast(F32)
+            ro = ro_pool.tile([P, 2048], F32, name="ro", tag="ro")
+            ordered[i] = ro
+            for half in range(2):
+                cols = slice(1024 * half, 1024 * (half + 1))
+                nc.scalar.copy(
+                    out=ro[:, cols].rearrange("p (c u i) -> p c u i", c=4, u=2),
+                    in_=words[:, cols].rearrange("p (c i u) -> p c u i", c=4, u=2),
+                )
+
         def dummy_matmuls(n):
             acc = psum.tile([P, N_TILE], F32, name="acc", tag="acc")
             for rep in range(n):
@@ -161,7 +177,11 @@ def tile_vae_pb_kernel(tc, hd, W_mu_d, b_mu_d, W_ls_d, b_ls_d, eps_x, out):
                     else:
                         c = 4 * (b // 2) + 2 * (b % 2) + s
                     for u in range(2):
-                        nc.tensor.transpose(tp[:, s, u, :], words[:, 256 * c + u : 256 * (c + 1) : 2], ident[:])
+                        if i in ordered:
+                            src_w = ordered[i][:, 256 * c + 128 * u : 256 * c + 128 * (u + 1)]
+                        else:
+                            src_w = words[:, 256 * c + u : 256 * (c + 1) : 2]
+                        nc.tensor.transpose(tp[:, s, u, :], src_w, ident[:])
                 banks.append(tp)
             for b in range(4):
                 blk = 2 * (b % 2) + b // 2 if kind == "w" else b
@@ -172,6 +192,8 @@ def tile_vae_pb_kernel(tc, hd, W_mu_d, b_mu_d, W_ls_d, b_ls_d, eps_x, out):
                     nc.vector.tensor_copy(out=dst, in_=src)
                 else:
                     nc.scalar.copy(out=dst, in_=src)
+            if REORDER_FROM <= i + RO_AHEAD < len(RUNS):
+                reorder(i + RO_AHEAD)
             if kind == "w":
                 codes, scales, at = w_codes[a], w_scales[a], 1024 * kh
             else:

@@ -52,8 +52,6 @@ PASSES_AFTER_RUN = [
 EPS_AFTER_LOAD = {4: 0, 5: 1, 6: 2, 7: 3}
 RAW_BUFS = 6
 WARM = 6
-REORDER_FROM = 9
-RO_AHEAD = 2
 P_ON_GPSIMD = False
 Q_ON_GPSIMD = False
 
@@ -65,7 +63,6 @@ def tile_vae_pb_kernel(tc, hd, W_mu_d, b_mu_d, W_ls_d, b_ls_d, eps_x, out):
         keep = ctx.enter_context(tc.tile_pool(name="keep", bufs=1))
         raw_pool = ctx.enter_context(tc.tile_pool(name="rawp", bufs=RAW_BUFS))
         grp_pool = ctx.enter_context(tc.tile_pool(name="grpp", bufs=3))
-        ro_pool = ctx.enter_context(tc.tile_pool(name="rop", bufs=3))
         psum = ctx.enter_context(tc.psum_pool(name="psum", bufs=4))
         ctx.enter_context(tc.manual_schedule(engines={mybir.EngineType.PE, mybir.EngineType.SP}))
 
@@ -137,19 +134,6 @@ def tile_vae_pb_kernel(tc, hd, W_mu_d, b_mu_d, W_ls_d, b_ls_d, eps_x, out):
                     in_=eps_x[e * 2 * P : (e + 1) * 2 * P, :].rearrange("(a p) x -> p a x", p=P),
                 )
 
-        ordered = {}
-
-        def reorder(i):
-            words = raws[i][:].bitcast(F32)
-            ro = ro_pool.tile([P, 2048], F32, name="ro", tag="ro")
-            ordered[i] = ro
-            for half in range(2):
-                cols = slice(1024 * half, 1024 * (half + 1))
-                nc.scalar.copy(
-                    out=ro[:, cols].rearrange("p (c u i) -> p c u i", c=4, u=2),
-                    in_=words[:, cols].rearrange("p (c i u) -> p c u i", c=4, u=2),
-                )
-
         def dummy_matmuls(n):
             acc = psum.tile([P, N_TILE], F32, name="acc", tag="acc")
             for rep in range(n):
@@ -177,32 +161,28 @@ def tile_vae_pb_kernel(tc, hd, W_mu_d, b_mu_d, W_ls_d, b_ls_d, eps_x, out):
                     else:
                         c = 4 * (b // 2) + 2 * (b % 2) + s
                     for u in range(2):
-                        if i in ordered:
-                            src_w = ordered[i][:, 256 * c + 128 * u : 256 * c + 128 * (u + 1)]
-                        else:
-                            src_w = words[:, 256 * c + u : 256 * (c + 1) : 2]
-                        nc.tensor.transpose(tp[:, s, u, :], src_w, ident[:])
+                        nc.tensor.transpose(tp[:, s, u, :], words[:, 256 * c + u : 256 * (c + 1) : 2], ident[:])
                 banks.append(tp)
             for b in range(4):
                 blk = 2 * (b % 2) + b // 2 if kind == "w" else b
                 dst = grp[:, 1024 * blk : 1024 * (blk + 1)].bitcast(F32)
                 dst = dst.rearrange("p (s r u) -> p s r u", s=2, u=2)
                 src = banks[b][:].rearrange("p s u r -> p s r u")
-                if b in VECTOR_BANKS[i]:
-                    nc.vector.tensor_copy(out=dst, in_=src)
-                else:
-                    nc.scalar.copy(out=dst, in_=src)
-            if REORDER_FROM <= i + RO_AHEAD < len(RUNS):
-                reorder(i + RO_AHEAD)
+                with tc.high_priority():
+                    if b in VECTOR_BANKS[i]:
+                        nc.vector.tensor_copy(out=dst, in_=src)
+                    else:
+                        nc.scalar.copy(out=dst, in_=src)
             if kind == "w":
                 codes, scales, at = w_codes[a], w_scales[a], 1024 * kh
             else:
                 codes, scales, at = h_codes, h_scales, 1024 * a
-            nc.vector.quantize_mx(
-                out=codes[:, at : at + 1024].bitcast(FP8X4),
-                scales=scales[:, at : at + 1024],
-                in_=grp[:],
-            )
+            with tc.high_priority():
+                nc.vector.quantize_mx(
+                    out=codes[:, at : at + 1024].bitcast(FP8X4),
+                    scales=scales[:, at : at + 1024],
+                    in_=grp[:],
+                )
 
         def finish_ls(m, h):
             r = res[(m, h)]
@@ -235,11 +215,13 @@ def tile_vae_pb_kernel(tc, hd, W_mu_d, b_mu_d, W_ls_d, b_ls_d, eps_x, out):
             if kh == 0:
                 return
             if q in (LS0, LS1):
-                nc.vector.tensor_tensor(out=r[:], in0=acc[:], in1=bias[:, h * N_TILE : (h + 1) * N_TILE], op=ADD)
+                with tc.high_priority():
+                    nc.vector.tensor_tensor(out=r[:], in0=acc[:], in1=bias[:, h * N_TILE : (h + 1) * N_TILE], op=ADD)
                 nc.scalar.activation(out=r[:], in_=r[:], func=EXP, scale=0.5)
                 finish_ls(m, h)
             else:
-                nc.vector.tensor_tensor(out=r[:], in0=acc[:], in1=r[:], op=ADD)
+                with tc.high_priority():
+                    nc.vector.tensor_tensor(out=r[:], in0=acc[:], in1=r[:], op=ADD)
                 nc.sync.dma_start(out=out[m * P : (m + 1) * P, h * N_TILE : (h + 1) * N_TILE], in_=r[:])
 
         for i in range(RAW_BUFS):

@@ -50,7 +50,9 @@ PASSES_AFTER_RUN = [
     halves((4, 5, 6, 7), MU0, (0, 1)) + halves((0, 1, 2, 3), MU1, (0, 1)) + halves((4, 5, 6, 7), MU1, (0, 1)),
 ]
 EPS_AFTER_LOAD = {4: 0, 5: 1, 6: 2, 7: 3}
-RAW_BUFS = 6
+RAW_BUFS = 4
+REORDER_FROM = 10
+RO_AHEAD = 2
 WARM = 6
 P_ON_GPSIMD = False
 Q_ON_GPSIMD = False
@@ -134,6 +136,19 @@ def tile_vae_pb_kernel(tc, hd, W_mu_d, b_mu_d, W_ls_d, b_ls_d, eps_x, out):
                     in_=eps_x[e * 2 * P : (e + 1) * 2 * P, :].rearrange("(a p) x -> p a x", p=P),
                 )
 
+        ordered = {}
+
+        def reorder(i):
+            words = raws[i][:].bitcast(F32)
+            ro = raw_pool.tile([P, 2048], F32, name="ro", tag="raw")
+            ordered[i] = ro
+            for half in range(2):
+                cols = slice(1024 * half, 1024 * (half + 1))
+                nc.scalar.copy(
+                    out=ro[:, cols].rearrange("p (c u i) -> p c u i", c=4, u=2),
+                    in_=words[:, cols].rearrange("p (c i u) -> p c u i", c=4, u=2),
+                )
+
         def dummy_matmuls(n):
             acc = psum.tile([P, N_TILE], F32, name="acc", tag="acc")
             for rep in range(n):
@@ -161,7 +176,11 @@ def tile_vae_pb_kernel(tc, hd, W_mu_d, b_mu_d, W_ls_d, b_ls_d, eps_x, out):
                     else:
                         c = 4 * (b // 2) + 2 * (b % 2) + s
                     for u in range(2):
-                        nc.tensor.transpose(tp[:, s, u, :], words[:, 256 * c + u : 256 * (c + 1) : 2], ident[:])
+                        if i in ordered:
+                            src_w = ordered[i][:, 256 * c + 128 * u : 256 * c + 128 * (u + 1)]
+                        else:
+                            src_w = words[:, 256 * c + u : 256 * (c + 1) : 2]
+                        nc.tensor.transpose(tp[:, s, u, :], src_w, ident[:])
                 banks.append(tp)
             for b in range(4):
                 blk = 2 * (b % 2) + b // 2 if kind == "w" else b
@@ -173,6 +192,8 @@ def tile_vae_pb_kernel(tc, hd, W_mu_d, b_mu_d, W_ls_d, b_ls_d, eps_x, out):
                         nc.vector.tensor_copy(out=dst, in_=src)
                     else:
                         nc.scalar.copy(out=dst, in_=src)
+            if REORDER_FROM <= i + RO_AHEAD < len(RUNS):
+                reorder(i + RO_AHEAD)
             if kind == "w":
                 codes, scales, at = w_codes[a], w_scales[a], 1024 * kh
             else:

@@ -54,8 +54,7 @@ RAW_BUFS = 4
 REORDER_FROM = 10
 RO_AHEAD = 2
 WARM = 6
-P_ON_GPSIMD = False
-Q_ON_GPSIMD = False
+B_LAG = 1
 
 
 def tile_vae_pb_kernel(tc, hd, W_mu_d, b_mu_d, W_ls_d, b_ls_d, eps_x, out):
@@ -205,12 +204,20 @@ def tile_vae_pb_kernel(tc, hd, W_mu_d, b_mu_d, W_ls_d, b_ls_d, eps_x, out):
                     in_=grp[:],
                 )
 
+        waiting = []
+
+        def add_b_mu(keep_back):
+            while len(waiting) > keep_back:
+                m, h = waiting[0]
+                waiting.remove((m, h))
+                r = res[(m, h)]
+                nc.vector.tensor_tensor(out=r[:], in0=r[:], in1=bias[:, XO + h * N_TILE : XO + (h + 1) * N_TILE], op=ADD)
+
         def finish_ls(m, h):
             r = res[(m, h)]
-            pe = nc.gpsimd if P_ON_GPSIMD else nc.vector
-            qe = nc.gpsimd if Q_ON_GPSIMD else nc.vector
-            pe.tensor_tensor(out=r[:], in0=r[:], in1=eps_sb[m // 2][:, m % 2, h * N_TILE : (h + 1) * N_TILE], op=MULT)
-            qe.tensor_tensor(out=r[:], in0=r[:], in1=bias[:, XO + h * N_TILE : XO + (h + 1) * N_TILE], op=ADD)
+            nc.vector.tensor_tensor(out=r[:], in0=r[:], in1=eps_sb[m // 2][:, m % 2, h * N_TILE : (h + 1) * N_TILE], op=MULT)
+            waiting.append((m, h))
+            add_b_mu(B_LAG)
 
         accs = {}
 
@@ -241,6 +248,7 @@ def tile_vae_pb_kernel(tc, hd, W_mu_d, b_mu_d, W_ls_d, b_ls_d, eps_x, out):
                 nc.scalar.activation(out=r[:], in_=r[:], func=EXP, scale=0.5)
                 finish_ls(m, h)
             else:
+                add_b_mu(0)
                 with tc.high_priority():
                     nc.vector.tensor_tensor(out=r[:], in0=acc[:], in1=r[:], op=ADD)
                 nc.sync.dma_start(out=out[m * P : (m + 1) * P, h * N_TILE : (h + 1) * N_TILE], in_=r[:])

@@ -43,11 +43,11 @@ PASSES_AFTER_RUN = [
     halves((0, 1), LS1, (0,)),
     halves((0, 1), LS1, (1,)),
     whole([(2, LS0), (3, LS0), (2, LS1)]),
-    whole([(3, LS1), (4, LS0), (5, LS0)]),
-    whole([(4, LS1), (5, LS1), (6, LS0)]),
-    whole([(7, LS0), (6, LS1), (7, LS1)]),
-    halves((0, 1, 2, 3), MU0, (0, 1)),
-    halves((4, 5, 6, 7), MU0, (0, 1)) + halves((0, 1, 2, 3), MU1, (0, 1)) + halves((4, 5, 6, 7), MU1, (0, 1)),
+    whole([(4, LS0), (5, LS0), (3, LS1)]),
+    whole([(6, LS0), (7, LS0), (4, LS1)]),
+    whole([(5, LS1), (6, LS1), (7, LS1)]),
+    whole([(0, MU0), (1, MU0), (2, MU0), (3, MU0)]),
+    whole([(4, MU0), (5, MU0), (6, MU0), (7, MU0)]) + whole([(m, MU1) for m in range(8)]),
 ]
 EPS_AFTER_LOAD = {4: 0, 5: 1, 6: 2, 7: 3}
 RAW_BUFS = 4

@@ -121,11 +121,9 @@ def tile_vae_pb_kernel(tc, hd, W_mu_d, b_mu_d, W_ls_d, b_ls_d, eps_x, out):
                 r0 = (a % 2) * N_TILE
                 src = mat[r0 : r0 + N_TILE, kh * 1024 : (kh + 1) * 1024].rearrange("(j p) k -> p j k", p=P)
                 dst = raw[:].rearrange("p (j k) -> p j k", j=4)
-                for jh in range(2) if n > 1 else ():
-                    js = slice(2 * jh, 2 * jh + 2)
-                    for c in range(n // 2):
-                        ks = slice(c * 2048 // n, (c + 1) * 2048 // n)
-                        nc.sync.dma_start(out=dst[:, js, ks], in_=src[:, js, ks])
+                for jp in range(n) if n > 1 else ():
+                    js = slice(jp * 4 // n, (jp + 1) * 4 // n)
+                    nc.sync.dma_start(out=dst[:, js, :], in_=src[:, js, :])
             if n == 1:
                 nc.sync.dma_start(out=dst, in_=src)
             if i in EPS_AFTER_LOAD:
@@ -169,18 +167,22 @@ def tile_vae_pb_kernel(tc, hd, W_mu_d, b_mu_d, W_ls_d, b_ls_d, eps_x, out):
             banks = []
             for b in range(4):
                 tp = psum.tile([P, 2, 2, P], F32, name="tp", tag="tp")
-                for s in range(2):
-                    if kind == "w":
-                        c = 4 * (b // 2) + 2 * s + b % 2
-                    else:
-                        c = 4 * (b // 2) + 2 * (b % 2) + s
-                    for u in range(2):
-                        if i in ordered:
-                            src_w = ordered[i][:, 256 * c + 128 * u : 256 * c + 128 * (u + 1)]
-                        else:
-                            src_w = words[:, 256 * c + u : 256 * (c + 1) : 2]
-                        nc.tensor.transpose(tp[:, s, u, :], src_w, ident[:])
                 banks.append(tp)
+            if kind == "w" and LOAD_SPLIT[i] < 4:
+                chunks = (0, 2, 1, 3, 4, 6, 5, 7)
+            else:
+                chunks = (0, 1, 2, 3, 4, 5, 6, 7)
+            for c in chunks:
+                if kind == "w":
+                    b, s = 2 * (c // 4) + c % 2, (c // 2) % 2
+                else:
+                    b, s = c // 2, c % 2
+                for u in range(2):
+                    if i in ordered:
+                        src_w = ordered[i][:, 256 * c + 128 * u : 256 * c + 128 * (u + 1)]
+                    else:
+                        src_w = words[:, 256 * c + u : 256 * (c + 1) : 2]
+                    nc.tensor.transpose(banks[b][:, s, u, :], src_w, ident[:])
             for b in range(4):
                 blk = 2 * (b % 2) + b // 2 if kind == "w" else b
                 dst = grp[:, 1024 * blk : 1024 * (blk + 1)].bitcast(F32)
@@ -249,9 +251,14 @@ def tile_vae_pb_kernel(tc, hd, W_mu_d, b_mu_d, W_ls_d, b_ls_d, eps_x, out):
                 finish_ls(m, h)
             else:
                 add_b_mu(0)
-                with tc.high_priority():
-                    nc.vector.tensor_tensor(out=r[:], in0=acc[:], in1=r[:], op=ADD)
-                nc.sync.dma_start(out=out[m * P : (m + 1) * P, h * N_TILE : (h + 1) * N_TILE], in_=r[:])
+                pieces = 2 if (m, q) == (7, MU1) else 1
+                for pc in range(pieces):
+                    cs = slice(pc * N_TILE // pieces, (pc + 1) * N_TILE // pieces)
+                    with tc.high_priority():
+                        nc.vector.tensor_tensor(out=r[:, cs], in0=acc[:, cs], in1=r[:, cs], op=ADD)
+                    nc.sync.dma_start(
+                        out=out[m * P : (m + 1) * P, h * N_TILE + cs.start : h * N_TILE + cs.stop], in_=r[:, cs]
+                    )
 
         for i in range(RAW_BUFS):
             load(i)

from contextlib import ExitStack

import concourse.masks as masks
import concourse.mybir as mybir

B, K, XO = 1024, 2048, 1024
FLOPS = 2 * 2 * B * K * XO

F32 = mybir.dt.float32
BF16 = mybir.dt.bfloat16
U32 = mybir.dt.uint32
U8 = mybir.dt.uint8
FP8X4 = mybir.dt.float8_e5m2_x4
ADD = mybir.AluOpType.add
MULT = mybir.AluOpType.mult
EXP = mybir.ActivationFunctionType.Exp

P = 128
N_TILE = 512

LS0, LS1, MU0, MU1 = 0, 1, 2, 3


def halves(ms, q, khs):
    return [(m, q, kh) for kh in khs for m in ms]


def whole(pairs):
    return [(m, q, kh) for (m, q) in pairs for kh in (0, 1)]


RUNS = [
    ("w", LS0, 0), ("h", 0, 0), ("w", LS0, 1), ("w", LS1, 0), ("w", LS1, 1), ("h", 1, 0),
    ("h", 2, 0), ("h", 3, 0), ("w", MU0, 0), ("w", MU0, 1), ("w", MU1, 0), ("w", MU1, 1),
]
LOAD_SPLIT = [4, 2, 2, 1, 1, 1, 1, 1, 1, 1, 1, 1]
VECTOR_BANKS = [(1,)] * 3 + [()] * 9
PASSES_AFTER_RUN = [
    [],
    [],
    halves((0, 1), LS0, (0,)),
    halves((0, 1), LS0, (1,)),
    halves((0, 1), LS1, (0,)),
    halves((0, 1), LS1, (1,)),
    whole([(2, LS0), (3, LS0), (2, LS1)]),
    whole([(4, LS0), (5, LS0), (3, LS1)]),
    whole([(6, LS0), (7, LS0), (4, LS1)]),
    whole([(5, LS1), (6, LS1), (7, LS1)]),
    whole([(0, MU0), (1, MU0), (2, MU0), (3, MU0)]),
    whole([(4, MU0), (5, MU0), (6, MU0), (7, MU0)]) + whole([(m, MU1) for m in range(8)]),
]
EPS_AFTER_LOAD = {4: 0, 5: 1, 6: 2, 7: 3}
RAW_BUFS = 4
REORDER_FROM = 10
RO_AHEAD = 2
WARM = 6
B_LAG = 1


def tile_vae_pb_kernel(tc, hd, W_mu_d, b_mu_d, W_ls_d, b_ls_d, eps_x, out):
    nc = tc.nc
    with ExitStack() as ctx:
        const = ctx.enter_context(tc.tile_pool(name="const", bufs=1))
        keep = ctx.enter_context(tc.tile_pool(name="keep", bufs=1))
        raw_pool = ctx.enter_context(tc.tile_pool(name="rawp", bufs=RAW_BUFS))
        grp_pool = ctx.enter_context(tc.tile_pool(name="grpp", bufs=3))
        psum = ctx.enter_context(tc.psum_pool(name="psum", bufs=4))
        ctx.enter_context(tc.manual_schedule(engines={mybir.EngineType.PE, mybir.EngineType.SP}))

        ident = const.tile([P, P], F32, name="ident")
        ones = const.tile([P, P], BF16, name="ones")
        warm = const.tile([P, N_TILE], BF16, name="warm")
        brow = const.tile([P, 2 * XO], BF16, name="brow")
        bias = const.tile([P, 2 * XO], F32, name="bias")
        tiny = const.tile([P, 2], F32, name="tiny")

        h_codes = keep.tile([P, 4096], U32, name="h_codes", align_bytes=64)
        h_scales = keep.tile([P, 4096], U8, name="h_scales", align_bytes=64)
        w_codes = []
        w_scales = []
        for q in range(4):
            wc = keep.tile([P, 2048], U32, name="w_codes%d" % q, align_bytes=64)
            ws = keep.tile([P, 2048], U8, name="w_scales%d" % q, align_bytes=64)
            w_codes.append(wc)
            w_scales.append(ws)
        eps_sb = []
        for e in range(4):
            et = keep.tile([P, 2, XO], BF16, name="eps%d" % e)
            eps_sb.append(et)
        res = {}
        for m in range(8):
            for h in range(2):
                rt = keep.tile([P, N_TILE], F32, name="res%d_%d" % (m, h))
                res[(m, h)] = rt

        nc.vector.memset(ones[:], 1.0)
        nc.vector.memset(warm[:], 0.0)
        nc.vector.memset(tiny[:], 0.0)
        nc.vector.memset(brow[:], 0.0)
        masks.make_identity(nc, ident[:])
        nc.scalar.dma_start(out=brow[0:1, 0:XO], in_=b_ls_d.rearrange("(o n) -> o n", o=1))
        nc.scalar.dma_start(out=brow[0:1, XO : 2 * XO], in_=b_mu_d.rearrange("(o n) -> o n", o=1))
        nc.scalar.activation(out=tiny[:, 1:2], in_=tiny[:, 0:1], func=EXP)

        raws = {}

        def load(i):
            kind, a, kh = RUNS[i]
            raw = raw_pool.tile([P, 4096], BF16, name="raw", tag="raw")
            raws[i] = raw
            n = LOAD_SPLIT[i]
            if kind == "h":
                src = hd[a * 2 * P : (a + 1) * 2 * P, :].rearrange("(j p) k -> p j k", p=P)
                dst = raw[:].rearrange("p (j k) -> p j k", j=2)
                for jj in range(2) if n > 1 else ():
                    for c in range(n // 2):
                        ks = slice(c * 2 * K // n, (c + 1) * 2 * K // n)
                        nc.sync.dma_start(out=dst[:, jj, ks], in_=src[:, jj, ks])
            else:
                mat = W_ls_d if a in (LS0, LS1) else W_mu_d
                r0 = (a % 2) * N_TILE
                src = mat[r0 : r0 + N_TILE, kh * 1024 : (kh + 1) * 1024].rearrange("(j p) k -> p j k", p=P)
                dst = raw[:].rearrange("p (j k) -> p j k", j=4)
                for jp in range(n) if n > 1 else ():
                    js = slice(jp * 4 // n, (jp + 1) * 4 // n)
                    nc.sync.dma_start(out=dst[:, js, :], in_=src[:, js, :])
            if n == 1:
                nc.sync.dma_start(out=dst, in_=src)
            if i in EPS_AFTER_LOAD:
                e = EPS_AFTER_LOAD[i]
                nc.sync.dma_start(
                    out=eps_sb[e][:],
                    in_=eps_x[e * 2 * P : (e + 1) * 2 * P, :].rearrange("(a p) x -> p a x", p=P),
                )

        ordered = {}

        def reorder(i):
            words = raws[i][:].bitcast(F32)
            ro = raw_pool.tile([P, 2048], F32, name="ro", tag="raw")
            ordered[i] = ro
            for half in range(2):
                cols = slice(1024 * half, 1024 * (half + 1))
                nc.scalar.copy(
                    out=ro[:, cols].rearrange("p (c u i) -> p c u i", c=4, u=2),
                    in_=words[:, cols].rearrange("p (c i u) -> p c u i", c=4, u=2),
                )

        def dummy_matmuls(n):
            acc = psum.tile([P, N_TILE], F32, name="acc", tag="acc")
            for rep in range(n):
                nc.tensor.matmul(out=acc[:], lhsT=ones[:], rhs=warm[:], start=True, stop=True)

        def bias_broadcast(c, engine):
            acc = psum.tile([P, N_TILE], F32, name="acc", tag="acc")
            cols = slice(c * N_TILE, (c + 1) * N_TILE)
            nc.tensor.matmul(out=acc[:], lhsT=ones[:], rhs=brow[:, cols], start=True, stop=True)
            if engine == "v":
                nc.vector.tensor_copy(out=bias[:, cols], in_=acc[:])
            else:
                nc.scalar.copy(out=bias[:, cols], in_=acc[:])

        def transpose_run(i):
            kind, a, kh = RUNS[i]
            words = raws[i][:].bitcast(F32)
            grp = grp_pool.tile([P, 4096], BF16, name="grp", tag="grp", align_bytes=64)
            banks = []
            for b in range(4):
                tp = psum.tile([P, 2, 2, P], F32, name="tp", tag="tp")
                banks.append(tp)
            if kind == "w" and LOAD_SPLIT[i] < 4:
                chunks = (0, 2, 1, 3, 4, 6, 5, 7)
            else:
                chunks = (0, 1, 2, 3, 4, 5, 6, 7)
            for c in chunks:
                if kind == "w":
                    b, s = 2 * (c // 4) + c % 2, (c // 2) % 2
                else:
                    b, s = c // 2, c % 2
                for u in range(2):
                    if i in ordered:
                        src_w = ordered[i][:, 256 * c + 128 * u : 256 * c + 128 * (u + 1)]
                    else:
                        src_w = words[:, 256 * c + u : 256 * (c + 1) : 2]
                    nc.tensor.transpose(banks[b][:, s, u, :], src_w, ident[:])
            for b in range(4):
                blk = 2 * (b % 2) + b // 2 if kind == "w" else b
                dst = grp[:, 1024 * blk : 1024 * (blk + 1)].bitcast(F32)
                dst = dst.rearrange("p (s r u) -> p s r u", s=2, u=2)
                src = banks[b][:].rearrange("p s u r -> p s r u")
                with tc.high_priority():
                    if b in VECTOR_BANKS[i]:
                        nc.vector.tensor_copy(out=dst, in_=src)
                    else:
                        nc.scalar.copy(out=dst, in_=src)
            if REORDER_FROM <= i + RO_AHEAD < len(RUNS):
                reorder(i + RO_AHEAD)
            if kind == "w":
                codes, scales, at = w_codes[a], w_scales[a], 1024 * kh
            else:
                codes, scales, at = h_codes, h_scales, 1024 * a
            with tc.high_priority():
                nc.vector.quantize_mx(
                    out=codes[:, at : at + 1024].bitcast(FP8X4),
                    scales=scales[:, at : at + 1024],
                    in_=grp[:],
                )

        waiting = []

        def add_b_mu(keep_back):
            while len(waiting) > keep_back:
                m, h = waiting[0]
                waiting.remove((m, h))
                r = res[(m, h)]
                nc.vector.tensor_tensor(out=r[:], in0=r[:], in1=bias[:, XO + h * N_TILE : XO + (h + 1) * N_TILE], op=ADD)

        def finish_ls(m, h):
            r = res[(m, h)]
            nc.vector.tensor_tensor(out=r[:], in0=r[:], in1=eps_sb[m // 2][:, m % 2, h * N_TILE : (h + 1) * N_TILE], op=MULT)
            waiting.append((m, h))
            add_b_mu(B_LAG)

        accs = {}

        def passes(m, q, kh):
            h = q % 2
            r = res[(m, h)]
            if kh == 0:
                acc = psum.tile([P, N_TILE], F32, name="acc", tag="acc")
                accs[(m, q)] = acc
            acc = accs[(m, q)]
            for g in (2 * kh, 2 * kh + 1):
                mc = slice(512 * m + P * g, 512 * m + P * (g + 1))
                nn = slice(N_TILE * g, N_TILE * (g + 1))
                nc.tensor.matmul_mx(
                    out=acc[:],
                    lhsT=h_codes[:, mc].bitcast(FP8X4),
                    lhsT_scale=h_scales[:, mc],
                    rhs=w_codes[q][:, nn].bitcast(FP8X4),
                    rhs_scale=w_scales[q][:, nn],
                    start=(g == 0),
                    stop=(g == 3),
                )
            if kh == 0:
                return
            if q in (LS0, LS1):
                with tc.high_priority():
                    nc.vector.tensor_tensor(out=r[:], in0=acc[:], in1=bias[:, h * N_TILE : (h + 1) * N_TILE], op=ADD)
                nc.scalar.activation(out=r[:], in_=r[:], func=EXP, scale=0.5)
                finish_ls(m, h)
            else:
                add_b_mu(0)
                pieces = 2 if (m, q) == (7, MU1) else 1
                for pc in range(pieces):
                    cs = slice(pc * N_TILE // pieces, (pc + 1) * N_TILE // pieces)
                    with tc.high_priority():
                        nc.vector.tensor_tensor(out=r[:, cs], in0=acc[:, cs], in1=r[:, cs], op=ADD)
                    nc.sync.dma_start(
                        out=out[m * P : (m + 1) * P, h * N_TILE + cs.start : h * N_TILE + cs.stop], in_=r[:, cs]
                    )

        for i in range(RAW_BUFS):
            load(i)
        dummy_matmuls(WARM)
        for i in range(len(RUNS)):
            if i >= 1 and i + RAW_BUFS - 1 < len(RUNS):
                load(i + RAW_BUFS - 1)
            transpose_run(i)
            if i == 0:
                bias_broadcast(0, "v")
                bias_broadcast(1, "s")
            if i == 1:
                bias_broadcast(2, "v")
                bias_broadcast(3, "s")
            for job in PASSES_AFTER_RUN[i]:
                passes(*job)
